import numpy as np
import ml_dtypes


def mxq(x, axis, fmt="e4m3"):
    dtype, down = {"e4m3": (ml_dtypes.float8_e4m3fn, 7), "e5m2": (ml_dtypes.float8_e5m2, 14)}[fmt]
    v = np.moveaxis(np.asarray(x, np.float32).astype(ml_dtypes.bfloat16).astype(np.float64), axis, -1)
    blocks = v.reshape(v.shape[:-1] + (-1, 32))
    amax = np.abs(blocks).max(-1, keepdims=True)
    byte = np.maximum(np.where(amax > 0, np.frexp(amax)[1] - 1 + 127, 0) - down, 1)
    scale = np.exp2(byte - 127.0)
    codes = (blocks / scale).astype(np.float32).astype(dtype).astype(np.float64)
    return np.moveaxis((codes * scale).reshape(v.shape), -1, axis)


WIDE = False


def mx_kscale(k):
    if not WIDE:
        return np.ones(k)
    levels = np.array([10, -10, 5, -5, 0])
    if k % 512:
        return np.exp2(np.random.permutation(np.resize(levels, k // 32))).repeat(32)
    a = np.empty((k // 512, 16))
    for p in range(k // 512):
        a[p, :8] = np.random.permutation(np.resize(levels, 8))
        for g in range(8):
            far = levels[np.abs(levels - a[p, g]) >= 10]
            a[p, g + 8] = far[np.random.randint(len(far))]
    return np.exp2(a.ravel()).repeat(32)


BF16 = ml_dtypes.bfloat16


def bf(x):
    return np.asarray(x, np.float32).astype(BF16)


def f64(x):
    return np.asarray(x).astype(np.float64)


B, N, DIN, DH, DOUT = 256, 4, 512, 512, 512
EPS = 1e-5


def elu(v):
    return np.where(v > 0.0, v, np.expm1(np.minimum(v, 0.0)))


def sigmoid(v):
    return 1.0 / (1.0 + np.exp(-v))


def setup_inputs():
    rn = np.random.standard_normal
    s, t = mx_kscale(DH), mx_kscale(DOUT)
    z = rn((B, N, DOUT))
    e = np.exp(z - z.max(1, keepdims=True))
    return {
        "hv": bf(elu(rn((B, N, DH))) * s),
        "x": bf(rn((B, N, DIN)) + 0.5),
        "sel_w": bf(e / e.sum(1, keepdims=True)),
        "vW1": bf(rn((N, DH, DOUT)) * 1.2 / np.sqrt(DH) / s[:, None] * t),
        "vb1": bf(rn((N, DOUT)) * 0.3 * t),
        "vW4": bf(rn((N, DOUT, DOUT)) / np.sqrt(DOUT) / t[:, None]),
        "vb4": bf(rn((N, DOUT)) * 0.3),
        "vW5": bf(rn((N, DOUT, DOUT)) / np.sqrt(DOUT) / t[:, None]),
        "vb5": bf(rn((N, DOUT)) * 0.3),
        "vlng": bf(1.0 + 0.2 * rn((N, DOUT))),
        "vlnb": bf(0.2 * rn((N, DOUT))),
    }


def reference(hv, x, sel_w, vW1, vb1, vW4, vb4, vW5, vb5, vlng, vlnb):
    hq = mxq(f64(hv).transpose(1, 0, 2), 2, "e4m3")
    e1v = (hq @ mxq(f64(vW1), 1, "e4m3")) + f64(vb1)[:, None, :]
    eq = mxq(e1v, 2, "e4m3")
    gv = sigmoid((eq @ mxq(f64(vW4), 1, "e4m3")) + f64(vb4)[:, None, :]) * ((eq @ mxq(f64(vW5), 1, "e4m3")) + f64(vb5)[:, None, :])
    r = f64(x) + gv.transpose(1, 0, 2)
    yv = (r - r.mean(-1, keepdims=True)) * (1.0 / np.sqrt(r.var(-1, keepdims=True) + EPS)) * f64(vlng) + f64(vlnb)
    return np.sum(f64(sel_w) * yv, axis=1)

@@ -1,0 +1,341 @@
+from contextlib import ExitStack
+
+import concourse.mybir as mybir
+from concourse.masks import make_identity
+
+F32 = mybir.dt.float32
+BF16 = mybir.dt.bfloat16
+U32 = mybir.dt.uint32
+U8 = mybir.dt.uint8
+FP8X4 = mybir.dt.float8_e4m3fn_x4
+ALU = mybir.AluOpType
+ACT = mybir.ActivationFunctionType
+
+P = 128
+PACK = 4
+B = 256
+NV = 4
+D = 512
+HALVES = B // P
+CHUNKS = D // P
+EPS = 1e-5
+BIAS_VECTORS = 2
+NORM_VECTORS = 2
+
+FLOPS = 3 * NV * 2 * B * D * D
+
+
+def tile_variableselectionnetwork_pb_kernel(
+    tc, hv, x, sel_w, vW1, vb1, vW4, vb4, vW5, vb5, vlng, vlnb, out
+):
+    nc = tc.nc
+    with ExitStack() as ctx:
+        consts = ctx.enter_context(tc.tile_pool(name="consts", bufs=1))
+        loads = ctx.enter_context(tc.tile_pool(name="loads", bufs=1))
+        quantised = ctx.enter_context(tc.tile_pool(name="quantised", bufs=1))
+        staging = ctx.enter_context(tc.tile_pool(name="staging", bufs=3))
+        work = ctx.enter_context(tc.tile_pool(name="work", bufs=4))
+        psum_stage1 = ctx.enter_context(tc.psum_pool(name="psum_stage1", bufs=2))
+        psum_gate = ctx.enter_context(tc.psum_pool(name="psum_gate", bufs=4))
+        psum_rows = ctx.enter_context(tc.psum_pool(name="psum_rows", bufs=2))
+
+        bias_rows = consts.tile([P, P], BF16)
+        nc.vector.memset(bias_rows[:], 0.0)
+        b1_cols = consts.tile([P, NV * PACK], BF16)
+
+        def load_bias_rows():
+            nc.sync.dma_start(
+                out=b1_cols[:].rearrange("p (n t) -> p n t", t=PACK),
+                in_=vb1.rearrange("n (p t) -> p n t", t=PACK),
+            )
+            for i, vec in enumerate((vb4, vb5, vlng, vlnb)):
+                nc.sync.dma_start(
+                    out=bias_rows[NV * CHUNKS * i : NV * CHUNKS * (i + 1), :],
+                    in_=vec.rearrange("n (c p) -> (n c) p", p=P),
+                )
+
+        def load_rows(src, name):
+            tiles = []
+            for h in range(HALVES):
+                t = loads.tile([P, NV * D], BF16, name="%s%d" % (name, h))
+                nc.sync.dma_start(
+                    out=t[:], in_=src[h * P : (h + 1) * P].rearrange("b n d -> b (n d)")
+                )
+                tiles.append(t)
+            return tiles
+
+        def load_w45(w, n, name):
+            t = loads.tile([P, PACK, D], BF16, name="%s_raw%d" % (name, n))
+            nc.sync.dma_start(out=t[:], in_=w[n].rearrange("(p t) c -> p t c", t=PACK))
+            return t
+
+        def load_w1(n):
+            return load_w45(vW1, n, "w1")
+
+        w1_raw, w4_raw, w5_raw = {}, {}, {}
+        load_bias_rows()
+        w1_raw[0] = load_w1(0)
+        hv_sb = load_rows(hv, "hv")
+        w4_raw[0] = load_w45(vW4, 0, "w4")
+        w5_raw[0] = load_w45(vW5, 0, "w5")
+        w1_raw[1] = load_w1(1)
+        w4_raw[1] = load_w45(vW4, 1, "w4")
+        w5_raw[1] = load_w45(vW5, 1, "w5")
+        w1_raw[2] = load_w1(2)
+        x_sb = load_rows(x, "x")
+        w4_raw[2] = load_w45(vW4, 2, "w4")
+        w5_raw[2] = load_w45(vW5, 2, "w5")
+        sel_sb = load_rows(sel_w, "sel")
+        w1_raw[3] = load_w1(3)
+        w4_raw[3] = load_w45(vW4, 3, "w4")
+        w5_raw[3] = load_w45(vW5, 3, "w5")
+
+        ident = consts.tile([P, P], F32)
+        make_identity(nc, ident[:])
+        ident_bf16 = consts.tile([P, P], BF16)
+        make_identity(nc, ident_bf16[:])
+        minus_half = consts.tile([P, HALVES], F32)
+        nc.gpsimd.memset(minus_half[:], -0.5)
+
+        table_warm = consts.tile([P, 1], F32)
+        nc.scalar.activation(out=table_warm[:], in_=minus_half[:, 0:1], func=ACT.Sigmoid)
+
+        bias_cols = consts.tile([P, BIAS_VECTORS * NV * CHUNKS], F32)
+        norm_cols = consts.tile([P, NORM_VECTORS * NV * CHUNKS], BF16)
+
+        def bias_col(i, n, c):
+            j = NV * CHUNKS * i + CHUNKS * n + c
+            return bias_cols[:, j : j + 1]
+
+        def spread_over_partitions(i, name):
+            spread = consts.tile([P, NV * D], BF16, name=name)
+            blocks_per_bank = 2 * D // P
+            for bank in range(NV * CHUNKS // blocks_per_bank):
+                spread_ps = psum_gate.tile([P, 2 * D], BF16, tag="gate")
+                for b in range(blocks_per_bank):
+                    j = NV * CHUNKS * i + blocks_per_bank * bank + b
+                    nc.tensor.transpose(
+                        spread_ps[:, b * P : (b + 1) * P],
+                        norm_cols[:, j : j + 1].to_broadcast([P, P]),
+                        ident_bf16[:],
+                    )
+                nc.scalar.copy(out=spread[:, bank * 2 * D : (bank + 1) * 2 * D], in_=spread_ps[:])
+            return spread
+
+        row_sum = consts.tile([P, NV * HALVES], F32)
+        sq_sum = consts.tile([P, NV * HALVES], F32)
+        neg_mean = consts.tile([P, NV * HALVES], F32)
+        var_eps = consts.tile([P, NV * HALVES], F32)
+        rstd = consts.tile([P, NV * HALVES], F32)
+
+        acc = [consts.tile([P, D], F32, name="acc%d" % h) for h in range(HALVES)]
+
+        def quantise_weight(raw, name, n):
+            grouped = staging.tile([P, D, PACK], BF16, tag="grouped", align_bytes=64)
+            if name == "w1":
+                dst = grouped[:].rearrange("p (u m) t -> p u m t", u=PACK)
+                src = raw[:].rearrange("p t (m u) -> p u m t", u=PACK)
+            else:
+                dst = grouped[:].rearrange("p (c i) t -> p c t i", i=4)
+                src = raw[:].rearrange("p t (c i) -> p c t i", i=4)
+            if n == 0 or name == "w1":
+                nc.vector.tensor_copy(out=dst, in_=src)
+            else:
+                nc.scalar.copy(out=dst, in_=src)
+            codes = quantised.tile([P, D], U32, name="%s_codes%d" % (name, n), align_bytes=64)
+            scales = quantised.tile([P, D], U8, name="%s_scales%d" % (name, n), align_bytes=64)
+            nc.vector.quantize_mx(
+                out=codes[:].bitcast(FP8X4),
+                scales=scales[:],
+                in_=grouped[:].rearrange("p c t -> p (c t)"),
+            )
+            return codes, scales
+
+        def quantise_hv(n):
+            words_per_row = D // 2
+            hvT_ps = psum_stage1.tile([P, 2, B], F32, tag="stage1")
+            for u in range(2):
+                for h in range(HALVES):
+                    first = n * words_per_row
+                    nc.tensor.transpose(
+                        hvT_ps[:, u, h * P : (h + 1) * P],
+                        hv_sb[h][:].bitcast(F32)[:, first + u : first + words_per_row : 2],
+                        ident[:],
+                    )
+            grouped = staging.tile([P, B * PACK], BF16, tag="hv_grouped", align_bytes=64)
+            nc.scalar.copy(
+                out=grouped[:].bitcast(F32).rearrange("p (b u) -> p b u", u=2),
+                in_=hvT_ps[:].rearrange("p u b -> p b u"),
+            )
+            codes = quantised.tile([P, B], U32, name="hv_codes%d" % n, align_bytes=64)
+            scales = quantised.tile([P, B], U8, name="hv_scales%d" % n, align_bytes=64)
+            nc.vector.quantize_mx(out=codes[:].bitcast(FP8X4), scales=scales[:], in_=grouped[:])
+            return codes, scales
+
+        def first_product(n, w1_q, hv_q):
+            grouped = staging.tile([P, B, PACK], BF16, tag="e1_grouped", align_bytes=64)
+            for h in range(HALVES):
+                rows = slice(h * P, (h + 1) * P)
+                e1_ps = psum_stage1.tile([P, PACK, P], F32, tag="stage1")
+                for t in range(PACK):
+                    feats = slice(t * P, (t + 1) * P)
+                    nc.tensor.matmul_mx(
+                        out=e1_ps[:, t, :],
+                        lhsT=w1_q[0][:, feats].bitcast(FP8X4),
+                        lhsT_scale=w1_q[1][:, feats],
+                        rhs=hv_q[0][:, rows].bitcast(FP8X4),
+                        rhs_scale=hv_q[1][:, rows],
+                        start=True,
+                        stop=True,
+                    )
+                first = PACK * n
+                nc.vector.tensor_tensor(
+                    out=grouped[:, rows, :],
+                    in0=e1_ps[:].rearrange("p t b -> p b t"),
+                    in1=b1_cols[:, first : first + PACK].unsqueeze(1).to_broadcast([P, P, PACK]),
+                    op=ALU.add,
+                )
+            codes = staging.tile([P, B], U32, tag="e1_codes", align_bytes=64)
+            scales = staging.tile([P, B], U8, tag="e1_scales", align_bytes=64)
+            nc.vector.quantize_mx(
+                out=codes[:].bitcast(FP8X4),
+                scales=scales[:],
+                in_=grouped[:].rearrange("p b t -> p (b t)"),
+            )
+            return codes, scales
+
+        def gate(n, e1_q, w4_q, w5_q):
+            gvT = work.tile([P, CHUNKS, B], F32, tag="gvT", bufs=2)
+            for pair in range(CHUNKS // 2):
+                banks = []
+                for w_q in (w4_q, w5_q):
+                    g_ps = psum_gate.tile([P, 2, B], F32, tag="gate")
+                    for i in range(2):
+                        c = 2 * pair + i
+                        feats = slice(c * P, (c + 1) * P)
+                        nc.tensor.matmul_mx(
+                            out=g_ps[:, i, :],
+                            lhsT=w_q[0][:, feats].bitcast(FP8X4),
+                            lhsT_scale=w_q[1][:, feats],
+                            rhs=e1_q[0][:].bitcast(FP8X4),
+                            rhs_scale=e1_q[1][:],
+                            start=True,
+                            stop=True,
+                        )
+                    banks.append(g_ps)
+                sig = work.tile([P, 2, B], F32, tag="sig")
+                for i in range(2):
+                    c = 2 * pair + i
+                    nc.scalar.activation(
+                        out=sig[:, i, :], in_=banks[0][:, i, :], func=ACT.Sigmoid, bias=bias_col(0, n, c)
+                    )
+                    nc.vector.scalar_tensor_tensor(
+                        out=gvT[:, c, :],
+                        in0=banks[1][:, i, :],
+                        scalar=bias_col(1, n, c),
+                        in1=sig[:, i, :],
+                        op0=ALU.add,
+                        op1=ALU.mult,
+                    )
+            return gvT
+
+        def residual_and_statistics(n, gvT):
+            feats = slice(n * D, (n + 1) * D)
+            cols = slice(n * HALVES, (n + 1) * HALVES)
+            r = []
+            for h in range(HALVES):
+                r_ps = psum_rows.tile([P, D], F32, tag="r_ps")
+                nc.tensor.matmul(
+                    out=r_ps[:], lhsT=ident_bf16[:], rhs=x_sb[h][:, feats], start=True, stop=False
+                )
+                for c in range(CHUNKS):
+                    nc.tensor.matmul(
+                        out=r_ps[:, c * P : (c + 1) * P],
+                        lhsT=gvT[:, c, h * P : (h + 1) * P],
+                        rhs=ident[:],
+                        is_transpose=True,
+                        start=False,
+                        stop=(c == CHUNKS - 1),
+                    )
+                r_h = work.tile([P, D], F32, tag="r", bufs=NV * HALVES)
+                j = n * HALVES + h
+                nc.scalar.activation(
+                    out=r_h[:], in_=r_ps[:], func=ACT.Identity, accum_out=row_sum[:, j : j + 1]
+                )
+                r.append(r_h)
+            nc.gpsimd.tensor_scalar(
+                out=neg_mean[:, cols], in0=row_sum[:, cols],
+                scalar1=-1.0 / D, scalar2=0.0, op0=ALU.mult, op1=ALU.add,
+            )
+            for h in range(HALVES):
+                j = n * HALVES + h
+                squares = work.tile([P, D], BF16, tag="squares")
+                nc.scalar.activation(
+                    out=squares[:], in_=r[h][:], func=ACT.Square,
+                    bias=neg_mean[:, j : j + 1], accum_out=sq_sum[:, j : j + 1],
+                )
+            nc.gpsimd.tensor_scalar(
+                out=var_eps[:, cols], in0=sq_sum[:, cols],
+                scalar1=1.0 / D, scalar2=EPS, op0=ALU.mult, op1=ALU.add,
+            )
+            nc.gpsimd.tensor_tensor(
+                out=rstd[:, cols], in0=var_eps[:, cols], in1=minus_half[:], op=ALU.pow
+            )
+            return r
+
+        def normalise_and_add(n, r):
+            feats = slice(n * D, (n + 1) * D)
+            scaled, y, weighted = [], [], []
+            for h in range(HALVES):
+                j = n * HALVES + h
+                t = work.tile([P, D], F32, tag="scaled")
+                nc.vector.scalar_tensor_tensor(
+                    out=t[:], in0=r[h][:], scalar=neg_mean[:, j : j + 1], in1=gamma_bc[:, feats],
+                    op0=ALU.add, op1=ALU.mult,
+                )
+                scaled.append(t)
+            for h in range(HALVES):
+                j = n * HALVES + h
+                t = work.tile([P, D], F32, tag="y")
+                nc.vector.scalar_tensor_tensor(
+                    out=t[:], in0=scaled[h][:], scalar=rstd[:, j : j + 1], in1=beta_bc[:, feats],
+                    op0=ALU.mult, op1=ALU.add,
+                )
+                y.append(t)
+            for h in range(HALVES):
+                t = acc[h] if n == 0 else work.tile([P, D], F32, name="weighted", tag="weighted")
+                nc.vector.tensor_tensor(out=t[:], in0=y[h][:], in1=sel_sb[h][:, feats], op=ALU.mult)
+                weighted.append(t)
+            if n > 0:
+                for h in range(HALVES):
+                    nc.vector.tensor_tensor(
+                        out=acc[h][:], in0=acc[h][:], in1=weighted[h][:], op=ALU.add
+                    )
+
+        def products_and_statistics(n):
+            w1_q = quantise_weight(w1_raw[n], "w1", n)
+            e1_q = first_product(n, w1_q, hv_q[n])
+            w4_q = quantise_weight(w4_raw[n], "w4", n)
+            w5_q = quantise_weight(w5_raw[n], "w5", n)
+            gvT = gate(n, e1_q, w4_q, w5_q)
+            return residual_and_statistics(n, gvT)
+
+        cols_ps = psum_stage1.tile([P, P], BF16, tag="stage1")
+        nc.tensor.transpose(cols_ps[:], bias_rows[:], ident_bf16[:])
+        first_norm_col = BIAS_VECTORS * NV * CHUNKS
+        nc.vector.tensor_copy(out=bias_cols[:], in_=cols_ps[:, 0:first_norm_col])
+        nc.vector.tensor_copy(
+            out=norm_cols[:],
+            in_=cols_ps[:, first_norm_col : first_norm_col + NORM_VECTORS * NV * CHUNKS],
+        )
+        hv_q = [quantise_hv(n) for n in range(NV)]
+        r = [products_and_statistics(0)]
+        gamma_bc = spread_over_partitions(0, "gamma_bc")
+        beta_bc = spread_over_partitions(1, "beta_bc")
+        for n in range(1, NV):
+            r.append(products_and_statistics(n))
+        for n in range(NV):
+            normalise_and_add(n, r[n])
+
+        for h in range(HALVES):
+            nc.sync.dma_start(out=out[h * P : (h + 1) * P, :], in_=acc[h][:])

@@ -19,10 +19,21 @@ D = 512
 HALVES = B // P
 CHUNKS = D // P
 EPS = 1e-5
-BIAS_VECTORS = 2
-NORM_VECTORS = 2
+COLUMN_VECTORS = 4
+STATS = 6
 
 FLOPS = 3 * NV * 2 * B * D * D
+
+SEQ = "w10 w40 w50 hv0 hv1 hv2 hv3 s0 g0 w11 w41 w51 s1 g1 w12 w42 w52 s2 r0 g2 w13 w43 w53 s3 r1 g3 r2 b0 r3 b1 b2 b3 a0 a1 a2 a3"
+VECTOR_REGROUPS = tuple((s[:2], int(s[2])) for s in "w10 w50 w11 w12 w13 w41".split())
+GPSIMD_REGROUPS = tuple((s[:2], int(s[2])) for s in "".split())
+TAIL = 1
+HP = "".split()
+FIRST_ADDED = [int(s[1]) for s in SEQ.split() if s[0] == "a"][0]
+LAST_ADDED = [int(s[1]) for s in SEQ.split() if s[0] == "a"][-1]
+GP = 4
+PS_KIND = dict(s.split(":") for s in "hvT:a e1:a g:a r:a zT:a selT:a cols:a out:a;a=8".split(";")[0].split())
+PS_BUFS = dict((s.split("=")[0], int(s.split("=")[1])) for s in "hvT:a e1:a g:a r:a zT:a selT:a cols:a out:a;a=8".split(";")[1].split())
 
 
 def tile_variableselectionnetwork_pb_kernel(
@@ -34,23 +45,21 @@ def tile_variableselectionnetwork_pb_kernel(
         loads = ctx.enter_context(tc.tile_pool(name="loads", bufs=1))
         quantised = ctx.enter_context(tc.tile_pool(name="quantised", bufs=1))
         staging = ctx.enter_context(tc.tile_pool(name="staging", bufs=3))
-        work = ctx.enter_context(tc.tile_pool(name="work", bufs=4))
-        psum_stage1 = ctx.enter_context(tc.psum_pool(name="psum_stage1", bufs=2))
-        psum_gate = ctx.enter_context(tc.psum_pool(name="psum_gate", bufs=4))
-        psum_rows = ctx.enter_context(tc.psum_pool(name="psum_rows", bufs=2))
+        work = ctx.enter_context(tc.tile_pool(name="work", bufs=2))
+        psum = ctx.enter_context(tc.psum_pool(name="psum", bufs=6))
 
-        bias_rows = consts.tile([P, P], BF16)
-        nc.vector.memset(bias_rows[:], 0.0)
+        vector_rows = consts.tile([P, P], BF16)
+        nc.vector.memset(vector_rows[:], 0.0)
         b1_cols = consts.tile([P, NV * PACK], BF16)
 
-        def load_bias_rows():
+        def load_vectors():
             nc.sync.dma_start(
                 out=b1_cols[:].rearrange("p (n t) -> p n t", t=PACK),
                 in_=vb1.rearrange("n (p t) -> p n t", t=PACK),
             )
             for i, vec in enumerate((vb4, vb5, vlng, vlnb)):
                 nc.sync.dma_start(
-                    out=bias_rows[NV * CHUNKS * i : NV * CHUNKS * (i + 1), :],
+                    out=vector_rows[NV * CHUNKS * i : NV * CHUNKS * (i + 1), :],
                     in_=vec.rearrange("n (c p) -> (n c) p", p=P),
                 )
 
@@ -64,31 +73,26 @@ def tile_variableselectionnetwork_pb_kernel(
                 tiles.append(t)
             return tiles
 
-        def load_w45(w, n, name):
+        def load_weight(w, n, name):
             t = loads.tile([P, PACK, D], BF16, name="%s_raw%d" % (name, n))
             nc.sync.dma_start(out=t[:], in_=w[n].rearrange("(p t) c -> p t c", t=PACK))
             return t
 
-        def load_w1(n):
-            return load_w45(vW1, n, "w1")
-
         w1_raw, w4_raw, w5_raw = {}, {}, {}
-        load_bias_rows()
-        w1_raw[0] = load_w1(0)
-        hv_sb = load_rows(hv, "hv")
-        w4_raw[0] = load_w45(vW4, 0, "w4")
-        w5_raw[0] = load_w45(vW5, 0, "w5")
-        w1_raw[1] = load_w1(1)
-        w4_raw[1] = load_w45(vW4, 1, "w4")
-        w5_raw[1] = load_w45(vW5, 1, "w5")
-        w1_raw[2] = load_w1(2)
-        x_sb = load_rows(x, "x")
-        w4_raw[2] = load_w45(vW4, 2, "w4")
-        w5_raw[2] = load_w45(vW5, 2, "w5")
-        sel_sb = load_rows(sel_w, "sel")
-        w1_raw[3] = load_w1(3)
-        w4_raw[3] = load_w45(vW4, 3, "w4")
-        w5_raw[3] = load_w45(vW5, 3, "w5")
+        acts = {}
+        for item in "w10 w40 w50 w11 vec hv w41 w51 w12 x w42 w52 w13 sel w43 w53".split():
+            if item == "vec":
+                load_vectors()
+            elif item == "hv":
+                acts["hv"] = load_rows(hv, "hv")
+            elif item == "x":
+                acts["x"] = load_rows(x, "x")
+            elif item == "sel":
+                acts["sel"] = load_rows(sel_w, "sel")
+            else:
+                n = int(item[2])
+                {"w1": w1_raw, "w4": w4_raw, "w5": w5_raw}[item[:2]][n] = load_weight({"w1": vW1, "w4": vW4, "w5": vW5}[item[:2]], n, item[:2])
+        hv_sb, x_sb, sel_sb = acts["hv"], acts["x"], acts["sel"]
 
         ident = consts.tile([P, P], F32)
         make_identity(nc, ident[:])
@@ -100,45 +104,37 @@ def tile_variableselectionnetwork_pb_kernel(
         table_warm = consts.tile([P, 1], F32)
         nc.scalar.activation(out=table_warm[:], in_=minus_half[:, 0:1], func=ACT.Sigmoid)
 
-        bias_cols = consts.tile([P, BIAS_VECTORS * NV * CHUNKS], F32)
-        norm_cols = consts.tile([P, NORM_VECTORS * NV * CHUNKS], BF16)
+        vector_cols = consts.tile([P, COLUMN_VECTORS * NV * CHUNKS], F32)
 
-        def bias_col(i, n, c):
+        def column(i, n, c):
             j = NV * CHUNKS * i + CHUNKS * n + c
-            return bias_cols[:, j : j + 1]
+            return vector_cols[:, j : j + 1]
 
-        def spread_over_partitions(i, name):
-            spread = consts.tile([P, NV * D], BF16, name=name)
-            blocks_per_bank = 2 * D // P
-            for bank in range(NV * CHUNKS // blocks_per_bank):
-                spread_ps = psum_gate.tile([P, 2 * D], BF16, tag="gate")
-                for b in range(blocks_per_bank):
-                    j = NV * CHUNKS * i + blocks_per_bank * bank + b
-                    nc.tensor.transpose(
-                        spread_ps[:, b * P : (b + 1) * P],
-                        norm_cols[:, j : j + 1].to_broadcast([P, P]),
-                        ident_bf16[:],
-                    )
-                nc.scalar.copy(out=spread[:, bank * 2 * D : (bank + 1) * 2 * D], in_=spread_ps[:])
-            return spread
-
-        row_sum = consts.tile([P, NV * HALVES], F32)
-        sq_sum = consts.tile([P, NV * HALVES], F32)
+        mean_var = consts.tile([P, NV * HALVES, 2], F32)
         neg_mean = consts.tile([P, NV * HALVES], F32)
         var_eps = consts.tile([P, NV * HALVES], F32)
         rstd = consts.tile([P, NV * HALVES], F32)
+        neg_mean_rstd = consts.tile([P, NV * HALVES], F32)
 
-        acc = [consts.tile([P, D], F32, name="acc%d" % h) for h in range(HALVES)]
+        out_ps = []
 
         def quantise_weight(raw, name, n):
-            grouped = staging.tile([P, D, PACK], BF16, tag="grouped", align_bytes=64)
+            grouped = staging.tile([P, D, PACK], BF16, tag="grouped", bufs=6, align_bytes=64)
             if name == "w1":
                 dst = grouped[:].rearrange("p (u m) t -> p u m t", u=PACK)
                 src = raw[:].rearrange("p t (m u) -> p u m t", u=PACK)
             else:
                 dst = grouped[:].rearrange("p (c i) t -> p c t i", i=4)
                 src = raw[:].rearrange("p t (c i) -> p c t i", i=4)
-            if n == 0 or name == "w1":
+            if (name, n) in GPSIMD_REGROUPS:
+                if name != "w1":
+                    dst = grouped[:].rearrange("p (u m) t -> p u m t", u=GP)
+                    src = raw[:].rearrange("p t (u m) -> p u m t", u=GP)
+                for u in range(dst.shape[1]):
+                    nc.gpsimd.tensor_scalar(
+                        out=dst[:, u], in0=src[:, u], scalar1=1.0, scalar2=0.0, op0=ALU.mult, op1=ALU.add
+                    )
+            elif (name, n) in VECTOR_REGROUPS:
                 nc.vector.tensor_copy(out=dst, in_=src)
             else:
                 nc.scalar.copy(out=dst, in_=src)
@@ -153,7 +149,7 @@ def tile_variableselectionnetwork_pb_kernel(
 
         def quantise_hv(n):
             words_per_row = D // 2
-            hvT_ps = psum_stage1.tile([P, 2, B], F32, tag="stage1")
+            hvT_ps = psum.tile([P, 2, B], F32, name="hvT_ps", tag=PS_KIND["hvT"], bufs=PS_BUFS[PS_KIND["hvT"]])
             for u in range(2):
                 for h in range(HALVES):
                     first = n * words_per_row
@@ -176,7 +172,7 @@ def tile_variableselectionnetwork_pb_kernel(
             grouped = staging.tile([P, B, PACK], BF16, tag="e1_grouped", align_bytes=64)
             for h in range(HALVES):
                 rows = slice(h * P, (h + 1) * P)
-                e1_ps = psum_stage1.tile([P, PACK, P], F32, tag="stage1")
+                e1_ps = psum.tile([P, PACK, P], F32, name="e1_ps", tag=PS_KIND["e1"], bufs=PS_BUFS[PS_KIND["e1"]])
                 for t in range(PACK):
                     feats = slice(t * P, (t + 1) * P)
                     nc.tensor.matmul_mx(
@@ -205,11 +201,11 @@ def tile_variableselectionnetwork_pb_kernel(
             return codes, scales
 
         def gate(n, e1_q, w4_q, w5_q):
-            gvT = work.tile([P, CHUNKS, B], F32, tag="gvT", bufs=2)
+            gvT = work.tile([P, CHUNKS, B], F32, tag="gvT", bufs=NV)
             for pair in range(CHUNKS // 2):
                 banks = []
                 for w_q in (w4_q, w5_q):
-                    g_ps = psum_gate.tile([P, 2, B], F32, tag="gate")
+                    g_ps = psum.tile([P, 2, B], F32, name="g_ps", tag=PS_KIND["g"], bufs=PS_BUFS[PS_KIND["g"]])
                     for i in range(2):
                         c = 2 * pair + i
                         feats = slice(c * P, (c + 1) * P)
@@ -223,119 +219,169 @@ def tile_variableselectionnetwork_pb_kernel(
                             stop=True,
                         )
                     banks.append(g_ps)
-                sig = work.tile([P, 2, B], F32, tag="sig")
+                sig = work.tile([P, 2, B], F32, tag="sig", bufs=4)
                 for i in range(2):
                     c = 2 * pair + i
                     nc.scalar.activation(
-                        out=sig[:, i, :], in_=banks[0][:, i, :], func=ACT.Sigmoid, bias=bias_col(0, n, c)
+                        out=sig[:, i, :], in_=banks[0][:, i, :], func=ACT.Sigmoid, bias=column(0, n, c)
                     )
                     nc.vector.scalar_tensor_tensor(
                         out=gvT[:, c, :],
                         in0=banks[1][:, i, :],
-                        scalar=bias_col(1, n, c),
+                        scalar=column(1, n, c),
                         in1=sig[:, i, :],
                         op0=ALU.add,
                         op1=ALU.mult,
                     )
             return gvT
 
-        def residual_and_statistics(n, gvT):
+        def standardise(n, gvT):
             feats = slice(n * D, (n + 1) * D)
             cols = slice(n * HALVES, (n + 1) * HALVES)
-            r = []
+            r_ps = []
             for h in range(HALVES):
-                r_ps = psum_rows.tile([P, D], F32, tag="r_ps")
+                r_h = psum.tile([P, D], F32, name="r_ps", tag=PS_KIND["r"], bufs=PS_BUFS[PS_KIND["r"]])
                 nc.tensor.matmul(
-                    out=r_ps[:], lhsT=ident_bf16[:], rhs=x_sb[h][:, feats], start=True, stop=False
+                    out=r_h[:], lhsT=ident_bf16[:], rhs=x_sb[h][:, feats], start=True, stop=False
                 )
                 for c in range(CHUNKS):
                     nc.tensor.matmul(
-                        out=r_ps[:, c * P : (c + 1) * P],
+                        out=r_h[:, c * P : (c + 1) * P],
                         lhsT=gvT[:, c, h * P : (h + 1) * P],
                         rhs=ident[:],
                         is_transpose=True,
                         start=False,
                         stop=(c == CHUNKS - 1),
                     )
-                r_h = work.tile([P, D], F32, tag="r", bufs=NV * HALVES)
-                j = n * HALVES + h
-                nc.scalar.activation(
-                    out=r_h[:], in_=r_ps[:], func=ACT.Identity, accum_out=row_sum[:, j : j + 1]
-                )
-                r.append(r_h)
+                r_ps.append(r_h)
+                stats = work.tile([P, STATS], F32, tag="stats", bufs=4)
+                nc.vector.bn_stats(out=stats[:], in_=r_h[:])
+                nc.vector.bn_aggr(out=mean_var[:, n * HALVES + h, :], in_=stats[:])
             nc.gpsimd.tensor_scalar(
-                out=neg_mean[:, cols], in0=row_sum[:, cols],
-                scalar1=-1.0 / D, scalar2=0.0, op0=ALU.mult, op1=ALU.add,
+                out=var_eps[:, cols], in0=mean_var[:, cols, 1],
+                scalar1=1.0, scalar2=EPS, op0=ALU.mult, op1=ALU.add,
             )
-            for h in range(HALVES):
-                j = n * HALVES + h
-                squares = work.tile([P, D], BF16, tag="squares")
-                nc.scalar.activation(
-                    out=squares[:], in_=r[h][:], func=ACT.Square,
-                    bias=neg_mean[:, j : j + 1], accum_out=sq_sum[:, j : j + 1],
-                )
             nc.gpsimd.tensor_scalar(
-                out=var_eps[:, cols], in0=sq_sum[:, cols],
-                scalar1=1.0 / D, scalar2=EPS, op0=ALU.mult, op1=ALU.add,
+                out=neg_mean[:, cols], in0=mean_var[:, cols, 0],
+                scalar1=-1.0, scalar2=0.0, op0=ALU.mult, op1=ALU.add,
             )
             nc.gpsimd.tensor_tensor(
                 out=rstd[:, cols], in0=var_eps[:, cols], in1=minus_half[:], op=ALU.pow
             )
-            return r
+            nc.gpsimd.tensor_tensor(
+                out=neg_mean_rstd[:, cols], in0=neg_mean[:, cols], in1=rstd[:, cols], op=ALU.mult
+            )
+            z = []
+            for h in range(HALVES):
+                j = n * HALVES + h
+                z_h = work.tile([P, D], F32, tag="z", bufs=NV * HALVES)
+                if TAIL and n == NV - 1 and h == 1:
+                    nc.vector.tensor_scalar(
+                        out=z_h[:], in0=r_ps[h][:], scalar1=mean_var[:, j, 0:1], scalar2=rstd[:, j : j + 1],
+                        op0=ALU.subtract, op1=ALU.mult,
+                    )
+                else:
+                    nc.scalar.activation(
+                        out=z_h[:], in_=r_ps[h][:], func=ACT.Identity,
+                        scale=rstd[:, j : j + 1], bias=neg_mean_rstd[:, j : j + 1],
+                    )
+                z.append(z_h)
+            return z
 
-        def normalise_and_add(n, r):
-            feats = slice(n * D, (n + 1) * D)
-            scaled, y, weighted = [], [], []
-            for h in range(HALVES):
-                j = n * HALVES + h
-                t = work.tile([P, D], F32, tag="scaled")
-                nc.vector.scalar_tensor_tensor(
-                    out=t[:], in0=r[h][:], scalar=neg_mean[:, j : j + 1], in1=gamma_bc[:, feats],
-                    op0=ALU.add, op1=ALU.mult,
-                )
-                scaled.append(t)
-            for h in range(HALVES):
-                j = n * HALVES + h
-                t = work.tile([P, D], F32, tag="y")
-                nc.vector.scalar_tensor_tensor(
-                    out=t[:], in0=scaled[h][:], scalar=rstd[:, j : j + 1], in1=beta_bc[:, feats],
-                    op0=ALU.mult, op1=ALU.add,
-                )
-                y.append(t)
-            for h in range(HALVES):
-                t = acc[h] if n == 0 else work.tile([P, D], F32, name="weighted", tag="weighted")
-                nc.vector.tensor_tensor(out=t[:], in0=y[h][:], in1=sel_sb[h][:, feats], op=ALU.mult)
-                weighted.append(t)
-            if n > 0:
+        def weigh(n, z):
+            selT_ps = psum.tile([P, CHUNKS, B], BF16, name="selT_ps", tag=PS_KIND["selT"], bufs=PS_BUFS[PS_KIND["selT"]])
+            for c in range(CHUNKS):
                 for h in range(HALVES):
-                    nc.vector.tensor_tensor(
-                        out=acc[h][:], in0=acc[h][:], in1=weighted[h][:], op=ALU.add
+                    first = n * D + c * P
+                    nc.tensor.transpose(
+                        selT_ps[:, c, h * P : (h + 1) * P], sel_sb[h][:, first : first + P], ident_bf16[:]
+                    )
+            yT = work.tile([P, CHUNKS, B], F32, tag="yT", bufs=2)
+            for pair in range(CHUNKS // 2):
+                zT_ps = psum.tile([P, 2, B], F32, name="zT_ps", tag=PS_KIND["zT"], bufs=PS_BUFS[PS_KIND["zT"]])
+                for i in range(2):
+                    c = 2 * pair + i
+                    for h in range(HALVES):
+                        nc.tensor.transpose(
+                            zT_ps[:, i, h * P : (h + 1) * P], z[h][:, c * P : (c + 1) * P], ident[:]
+                        )
+                for i in range(2):
+                    c = 2 * pair + i
+                    if TAIL and n == NV - 1 and pair == 0:
+                        nc.vector.tensor_scalar(
+                            out=yT[:, c, :], in0=zT_ps[:, i, :], scalar1=column(2, n, c), scalar2=column(3, n, c),
+                            op0=ALU.mult, op1=ALU.add,
+                        )
+                    else:
+                        nc.scalar.activation(
+                            out=yT[:, c, :], in_=zT_ps[:, i, :], func=ACT.Identity,
+                            scale=column(2, n, c), bias=column(3, n, c),
+                        )
+            wT = work.tile([P, CHUNKS, B], F32, tag="wT", bufs=NV)
+            if TAIL and n == NV - 1:
+                for pair in range(CHUNKS // 2):
+                    cs = slice(2 * pair, 2 * pair + 2)
+                    nc.vector.tensor_tensor(out=wT[:, cs, :], in0=yT[:, cs, :], in1=selT_ps[:, cs, :], op=ALU.mult)
+            else:
+                nc.vector.tensor_tensor(out=wT[:], in0=yT[:], in1=selT_ps[:], op=ALU.mult)
+            return wT
+
+        def add_up(n, wT):
+            if not out_ps:
+                for h in range(HALVES):
+                    out_ps.append(psum.tile([P, D], F32, name="out_ps%d" % h, tag=PS_KIND["out"], bufs=PS_BUFS[PS_KIND["out"]]))
+            for h in range(HALVES):
+                for c in range(CHUNKS):
+                    nc.tensor.matmul(
+                        out=out_ps[h][:, c * P : (c + 1) * P],
+                        lhsT=wT[:, c, h * P : (h + 1) * P],
+                        rhs=ident[:],
+                        is_transpose=True,
+                        start=(n == FIRST_ADDED and c == 0),
+                        stop=(n == LAST_ADDED and c == CHUNKS - 1),
                     )
 
-        def products_and_statistics(n):
-            w1_q = quantise_weight(w1_raw[n], "w1", n)
-            e1_q = first_product(n, w1_q, hv_q[n])
-            w4_q = quantise_weight(w4_raw[n], "w4", n)
-            w5_q = quantise_weight(w5_raw[n], "w5", n)
-            gvT = gate(n, e1_q, w4_q, w5_q)
-            return residual_and_statistics(n, gvT)
+        ctx.enter_context(tc.manual_schedule(engines={mybir.EngineType.PE}))
+        cols_ps = psum.tile([P, P], BF16, name="cols_ps", tag=PS_KIND["cols"], bufs=PS_BUFS[PS_KIND["cols"]])
+        nc.tensor.transpose(cols_ps[:], vector_rows[:], ident_bf16[:])
+        nc.vector.tensor_copy(out=vector_cols[:], in_=cols_ps[:, 0 : COLUMN_VECTORS * NV * CHUNKS])
+        w_q, e1_q, gvT, z, wT = {}, {}, {}, {}, {}
 
-        cols_ps = psum_stage1.tile([P, P], BF16, tag="stage1")
-        nc.tensor.transpose(cols_ps[:], bias_rows[:], ident_bf16[:])
-        first_norm_col = BIAS_VECTORS * NV * CHUNKS
-        nc.vector.tensor_copy(out=bias_cols[:], in_=cols_ps[:, 0:first_norm_col])
-        nc.vector.tensor_copy(
-            out=norm_cols[:],
-            in_=cols_ps[:, first_norm_col : first_norm_col + NORM_VECTORS * NV * CHUNKS],
-        )
-        hv_q = [quantise_hv(n) for n in range(NV)]
-        r = [products_and_statistics(0)]
-        gamma_bc = spread_over_partitions(0, "gamma_bc")
-        beta_bc = spread_over_partitions(1, "beta_bc")
-        for n in range(1, NV):
-            r.append(products_and_statistics(n))
-        for n in range(NV):
-            normalise_and_add(n, r[n])
+        def prepare(n):
+            w_q["w1", n] = quantise_weight(w1_raw[n], "w1", n)
+            w_q["w4", n] = quantise_weight(w4_raw[n], "w4", n)
+            w_q["w5", n] = quantise_weight(w5_raw[n], "w5", n)
+
+        hv_q = {}
+        raws = {"w1": w1_raw, "w4": w4_raw, "w5": w5_raw}
+        def do_step(op, n):
+            if op in raws:
+                w_q[op, n] = quantise_weight(raws[op][n], op, n)
+            elif op == "hv":
+                hv_q[n] = quantise_hv(n)
+            elif op == "s":
+                e1_q[n] = first_product(n, w_q["w1", n], hv_q[n])
+            elif op == "g":
+                gvT[n] = gate(n, e1_q[n], w_q["w4", n], w_q["w5", n])
+            elif op == "r":
+                z[n] = standardise(n, gvT[n])
+            elif op == "b":
+                wT[n] = weigh(n, z[n])
+            elif op == "a":
+                add_up(n, wT[n])
+
+        for step in SEQ.split():
+            op, n = step[:-1], int(step[-1])
+            if op in HP:
+                with tc.high_priority():
+                    do_step(op, n)
+            else:
+                do_step(op, n)
 
         for h in range(HALVES):
-            nc.sync.dma_start(out=out[h * P : (h + 1) * P, :], in_=acc[h][:])
+            result = work.tile([P, D], F32, tag="result")
+            if h == 0:
+                nc.scalar.copy(out=result[:], in_=out_ps[h][:])
+            else:
+                nc.vector.tensor_copy(out=result[:], in_=out_ps[h][:])
+            nc.sync.dma_start(out=out[h * P : (h + 1) * P, :], in_=result[:])

@@ -121,8 +121,8 @@ def tile_variableselectionnetwork_pb_kernel(
         def quantise_weight(raw, name, n):
             grouped = staging.tile([P, D, PACK], BF16, tag="grouped", bufs=6, align_bytes=64)
             if name == "w1":
-                dst = grouped[:].rearrange("p (u m) t -> p u m t", u=PACK)
-                src = raw[:].rearrange("p t (m u) -> p u m t", u=PACK)
+                dst = grouped[:].rearrange("p (u m) t -> p m t u", u=PACK)
+                src = raw[:].rearrange("p t (m u) -> p m t u", u=PACK)
             else:
                 dst = grouped[:].rearrange("p (c i) t -> p c t i", i=4)
                 src = raw[:].rearrange("p t (c i) -> p c t i", i=4)
@@ -346,11 +346,6 @@ def tile_variableselectionnetwork_pb_kernel(
         nc.tensor.transpose(cols_ps[:], vector_rows[:], ident_bf16[:])
         nc.vector.tensor_copy(out=vector_cols[:], in_=cols_ps[:, 0 : COLUMN_VECTORS * NV * CHUNKS])
         w_q, e1_q, gvT, z, wT = {}, {}, {}, {}, {}
-
-        def prepare(n):
-            w_q["w1", n] = quantise_weight(w1_raw[n], "w1", n)
-            w_q["w4", n] = quantise_weight(w4_raw[n], "w4", n)
-            w_q["w5", n] = quantise_weight(w5_raw[n], "w5", n)
 
         hv_q = {}
         raws = {"w1": w1_raw, "w4": w4_raw, "w5": w5_raw}

@@ -51,12 +51,11 @@ def tile_variableselectionnetwork_pb_kernel(
         vector_rows = consts.tile([P, P], BF16)
         nc.vector.memset(vector_rows[:], 0.0)
         b1_cols = consts.tile([P, NV * PACK], BF16)
+        b1_rows = consts.tile([P, D], BF16)
+        nc.vector.memset(b1_rows[:], 0.0)
 
         def load_vectors():
-            nc.sync.dma_start(
-                out=b1_cols[:].rearrange("p (n t) -> p n t", t=PACK),
-                in_=vb1.rearrange("n (p t) -> p n t", t=PACK),
-            )
+            nc.sync.dma_start(out=b1_rows[0:NV, :], in_=vb1[:, :])
             for i, vec in enumerate((vb4, vb5, vlng, vlnb)):
                 nc.sync.dma_start(
                     out=vector_rows[NV * CHUNKS * i : NV * CHUNKS * (i + 1), :],
@@ -345,6 +344,13 @@ def tile_variableselectionnetwork_pb_kernel(
         cols_ps = psum.tile([P, P], BF16, name="cols_ps", tag=PS_KIND["cols"], bufs=PS_BUFS[PS_KIND["cols"]])
         nc.tensor.transpose(cols_ps[:], vector_rows[:], ident_bf16[:])
         nc.vector.tensor_copy(out=vector_cols[:], in_=cols_ps[:, 0 : COLUMN_VECTORS * NV * CHUNKS])
+        b1_ps = psum.tile([P, PACK, P], BF16, name="b1_ps", tag=PS_KIND["cols"], bufs=PS_BUFS[PS_KIND["cols"]])
+        for t in range(PACK):
+            nc.tensor.transpose(b1_ps[:, t, :], b1_rows[:, t:D:PACK], ident_bf16[:])
+        nc.vector.tensor_copy(
+            out=b1_cols[:].rearrange("p (n t) -> p n t", t=PACK),
+            in_=b1_ps[:, :, 0:NV].rearrange("p t n -> p n t"),
+        )
         w_q, e1_q, gvT, z, wT = {}, {}, {}, {}, {}
 
         hv_q = {}

@@ -27,11 +27,14 @@ FLOPS = 3 * NV * 2 * B * D * D
 SEQ = "w10 w40 w50 hv0 hv1 hv2 hv3 s0 g0 w11 w41 w51 s1 g1 w12 w42 w52 s2 r0 g2 w13 w43 w53 s3 r1 g3 r2 b0 r3 b1 b2 b3 a0 a1 a2 a3"
 VECTOR_REGROUPS = tuple((s[:2], int(s[2])) for s in "w10 w50 w11 w12 w13 w41".split())
 GPSIMD_REGROUPS = tuple((s[:2], int(s[2])) for s in "".split())
-TAIL = 1
+TAIL = 0
 HP = "".split()
 FIRST_ADDED = [int(s[1]) for s in SEQ.split() if s[0] == "a"][0]
 LAST_ADDED = [int(s[1]) for s in SEQ.split() if s[0] == "a"][-1]
 GP = 4
+ZV = "".split()
+AV = "".split()
+WP = "0 1 2 3".split()
 PS_KIND = dict(s.split(":") for s in "hvT:a e1:a g:a r:a zT:a selT:a cols:a out:a;a=8".split(";")[0].split())
 PS_BUFS = dict((s.split("=")[0], int(s.split("=")[1])) for s in "hvT:a e1:a g:a r:a zT:a selT:a cols:a out:a;a=8".split(";")[1].split())
 
@@ -256,11 +259,11 @@ def tile_variableselectionnetwork_pb_kernel(
                 stats = work.tile([P, STATS], F32, tag="stats", bufs=4)
                 nc.vector.bn_stats(out=stats[:], in_=r_h[:])
                 nc.vector.bn_aggr(out=mean_var[:, n * HALVES + h, :], in_=stats[:])
-            nc.gpsimd.tensor_scalar(
+            nc.vector.tensor_scalar(
                 out=var_eps[:, cols], in0=mean_var[:, cols, 1],
                 scalar1=1.0, scalar2=EPS, op0=ALU.mult, op1=ALU.add,
             )
-            nc.gpsimd.tensor_scalar(
+            nc.vector.tensor_scalar(
                 out=neg_mean[:, cols], in0=mean_var[:, cols, 0],
                 scalar1=-1.0, scalar2=0.0, op0=ALU.mult, op1=ALU.add,
             )
@@ -274,7 +277,7 @@ def tile_variableselectionnetwork_pb_kernel(
             for h in range(HALVES):
                 j = n * HALVES + h
                 z_h = work.tile([P, D], F32, tag="z", bufs=NV * HALVES)
-                if TAIL and n == NV - 1 and h == 1:
+                if str(n) in ZV and h == 1:
                     nc.vector.tensor_scalar(
                         out=z_h[:], in0=r_ps[h][:], scalar1=mean_var[:, j, 0:1], scalar2=rstd[:, j : j + 1],
                         op0=ALU.subtract, op1=ALU.mult,
@@ -306,7 +309,7 @@ def tile_variableselectionnetwork_pb_kernel(
                         )
                 for i in range(2):
                     c = 2 * pair + i
-                    if TAIL and n == NV - 1 and pair == 0:
+                    if str(n) in AV and pair == 0:
                         nc.vector.tensor_scalar(
                             out=yT[:, c, :], in0=zT_ps[:, i, :], scalar1=column(2, n, c), scalar2=column(3, n, c),
                             op0=ALU.mult, op1=ALU.add,
@@ -317,7 +320,7 @@ def tile_variableselectionnetwork_pb_kernel(
                             scale=column(2, n, c), bias=column(3, n, c),
                         )
             wT = work.tile([P, CHUNKS, B], F32, tag="wT", bufs=NV)
-            if TAIL and n == NV - 1:
+            if str(n) in WP:
                 for pair in range(CHUNKS // 2):
                     cs = slice(2 * pair, 2 * pair + 2)
                     nc.vector.tensor_tensor(out=wT[:, cs, :], in0=yT[:, cs, :], in1=selT_ps[:, cs, :], op=ALU.mult)

@@ -33,6 +33,7 @@ FIRST_ADDED = [int(s[1]) for s in SEQ.split() if s[0] == "a"][0]
 LAST_ADDED = [int(s[1]) for s in SEQ.split() if s[0] == "a"][-1]
 GP = 4
 ZV = "".split()
+ZF = "3".split()
 AV = "".split()
 WP = "0 1 2 3".split()
 PS_KIND = dict(s.split(":") for s in "hvT:a e1:a g:a r:a zT:a selT:a cols:a out:a;a=8".split(";")[0].split())
@@ -263,21 +264,23 @@ def tile_variableselectionnetwork_pb_kernel(
                 out=var_eps[:, cols], in0=mean_var[:, cols, 1],
                 scalar1=1.0, scalar2=EPS, op0=ALU.mult, op1=ALU.add,
             )
-            nc.vector.tensor_scalar(
-                out=neg_mean[:, cols], in0=mean_var[:, cols, 0],
-                scalar1=-1.0, scalar2=0.0, op0=ALU.mult, op1=ALU.add,
-            )
+            if str(n) not in ZF:
+                nc.vector.tensor_scalar(
+                    out=neg_mean[:, cols], in0=mean_var[:, cols, 0],
+                    scalar1=-1.0, scalar2=0.0, op0=ALU.mult, op1=ALU.add,
+                )
             nc.gpsimd.tensor_tensor(
                 out=rstd[:, cols], in0=var_eps[:, cols], in1=minus_half[:], op=ALU.pow
             )
-            nc.gpsimd.tensor_tensor(
-                out=neg_mean_rstd[:, cols], in0=neg_mean[:, cols], in1=rstd[:, cols], op=ALU.mult
-            )
+            if str(n) not in ZF:
+                nc.gpsimd.tensor_tensor(
+                    out=neg_mean_rstd[:, cols], in0=neg_mean[:, cols], in1=rstd[:, cols], op=ALU.mult
+                )
             z = []
             for h in range(HALVES):
                 j = n * HALVES + h
                 z_h = work.tile([P, D], F32, tag="z", bufs=NV * HALVES)
-                if str(n) in ZV and h == 1:
+                if str(n) in ZF or (str(n) in ZV and h == 1):
                     nc.vector.tensor_scalar(
                         out=z_h[:], in0=r_ps[h][:], scalar1=mean_var[:, j, 0:1], scalar2=rstd[:, j : j + 1],
                         op0=ALU.subtract, op1=ALU.mult,

@@ -24,7 +24,7 @@ STATS = 6
 
 FLOPS = 3 * NV * 2 * B * D * D
 
-SEQ = "w10 w40 w50 hv0 hv1 hv2 hv3 s0 g0 w11 w41 w51 s1 g1 w12 w42 w52 s2 r0 g2 w13 w43 w53 s3 r1 g3 r2 b0 r3 b1 b2 b3 a0 a1 a2 a3"
+SEQ = "w10 w40 w50 hv0 hv1 hv2 hv3 s0 g0 w11 w41 w51 s1 g1 w12 w42 w52 s2 r0 g2 w13 w43 w53 s3 r1 g3 r2 r3 b0 b1 b2 b3 a0 a1 a2 a3"
 VECTOR_REGROUPS = tuple((s[:2], int(s[2])) for s in "w10 w50 w11 w12 w13 w41".split())
 GPSIMD_REGROUPS = tuple((s[:2], int(s[2])) for s in "".split())
 TAIL = 0

@@ -127,8 +127,8 @@ def tile_variableselectionnetwork_pb_kernel(
                 dst = grouped[:].rearrange("p (u m) t -> p m t u", u=PACK)
                 src = raw[:].rearrange("p t (m u) -> p m t u", u=PACK)
             else:
-                dst = grouped[:].rearrange("p (c i) t -> p c t i", i=4)
-                src = raw[:].rearrange("p t (c i) -> p c t i", i=4)
+                dst = grouped[:].rearrange("p (c i) t -> p c t i", i=8)
+                src = raw[:].rearrange("p t (c i) -> p c t i", i=8)
             if (name, n) in GPSIMD_REGROUPS:
                 if name != "w1":
                     dst = grouped[:].rearrange("p (u m) t -> p u m t", u=GP)

@@ -118,6 +118,9 @@ def tile_variableselectionnetwork_pb_kernel(
         var_eps = consts.tile([P, NV * HALVES], F32)
         rstd = consts.tile([P, NV * HALVES], F32)
         neg_mean_rstd = consts.tile([P, NV * HALVES], F32)
+        rstd_late = consts.tile([P, NV * HALVES], F32)
+        neg_mean_rstd_late = consts.tile([P, NV * HALVES], F32)
+        table_warm_late = consts.tile([P, 1], F32)
 
         out_ps = []
 
@@ -236,6 +239,8 @@ def tile_variableselectionnetwork_pb_kernel(
                         op0=ALU.add,
                         op1=ALU.mult,
                     )
+            if n == NV - 1:
+                nc.scalar.activation(out=table_warm_late[:], in_=sig[:, 1, 0:1], func=ACT.Abs_reciprocal_sqrt)
             return gvT
 
         def standardise(n, gvT):
@@ -269,26 +274,39 @@ def tile_variableselectionnetwork_pb_kernel(
                     out=neg_mean[:, cols], in0=mean_var[:, cols, 0],
                     scalar1=-1.0, scalar2=0.0, op0=ALU.mult, op1=ALU.add,
                 )
-            nc.gpsimd.tensor_tensor(
-                out=rstd[:, cols], in0=var_eps[:, cols], in1=minus_half[:], op=ALU.pow
-            )
-            if str(n) not in ZF:
+            if n >= NV - 2:
+                nc.scalar.activation(out=rstd_late[:, cols], in_=var_eps[:, cols], func=ACT.Abs_reciprocal_sqrt)
+            else:
                 nc.gpsimd.tensor_tensor(
-                    out=neg_mean_rstd[:, cols], in0=neg_mean[:, cols], in1=rstd[:, cols], op=ALU.mult
+                    out=rstd[:, cols], in0=var_eps[:, cols], in1=minus_half[:], op=ALU.pow
                 )
+            if str(n) not in ZF:
+                if n >= NV - 2:
+                    for h in range(HALVES):
+                        j = n * HALVES + h
+                        nc.scalar.activation(
+                            out=neg_mean_rstd_late[:, j : j + 1], in_=neg_mean[:, j : j + 1], func=ACT.Identity,
+                            scale=rstd_late[:, j : j + 1],
+                        )
+                else:
+                    nc.gpsimd.tensor_tensor(
+                        out=neg_mean_rstd[:, cols], in0=neg_mean[:, cols], in1=rstd[:, cols], op=ALU.mult
+                    )
+            rstd_n = rstd_late if n >= NV - 2 else rstd
+            nms_n = neg_mean_rstd_late if n >= NV - 2 else neg_mean_rstd
             z = []
             for h in range(HALVES):
                 j = n * HALVES + h
                 z_h = work.tile([P, D], F32, tag="z", bufs=NV * HALVES)
                 if str(n) in ZF or (str(n) in ZV and h == 1):
                     nc.vector.tensor_scalar(
-                        out=z_h[:], in0=r_ps[h][:], scalar1=mean_var[:, j, 0:1], scalar2=rstd[:, j : j + 1],
+                        out=z_h[:], in0=r_ps[h][:], scalar1=mean_var[:, j, 0:1], scalar2=rstd_n[:, j : j + 1],
                         op0=ALU.subtract, op1=ALU.mult,
                     )
                 else:
                     nc.scalar.activation(
                         out=z_h[:], in_=r_ps[h][:], func=ACT.Identity,
-                        scale=rstd[:, j : j + 1], bias=neg_mean_rstd[:, j : j + 1],
+                        scale=rstd_n[:, j : j + 1], bias=nms_n[:, j : j + 1],
                     )
                 z.append(z_h)
             return z

from contextlib import ExitStack

import concourse.mybir as mybir
from concourse.masks import make_identity

F32 = mybir.dt.float32
BF16 = mybir.dt.bfloat16
U32 = mybir.dt.uint32
U8 = mybir.dt.uint8
FP8X4 = mybir.dt.float8_e4m3fn_x4
ALU = mybir.AluOpType
ACT = mybir.ActivationFunctionType

P = 128
PACK = 4
B = 256
NV = 4
D = 512
HALVES = B // P
CHUNKS = D // P
EPS = 1e-5
COLUMN_VECTORS = 4
STATS = 6

FLOPS = 3 * NV * 2 * B * D * D

SEQ = "w10 w40 w50 hv0 hv1 hv2 hv3 s0 g0 w11 w41 w51 s1 g1 w12 w42 w52 s2 r0 g2 w13 w43 w53 s3 r1 g3 r2 r3 b0 b1 b2 b3 a0 a1 a2 a3"
VECTOR_REGROUPS = tuple((s[:2], int(s[2])) for s in "w10 w50 w11 w12 w13 w41".split())
GPSIMD_REGROUPS = tuple((s[:2], int(s[2])) for s in "".split())
TAIL = 0
HP = "".split()
FIRST_ADDED = [int(s[1]) for s in SEQ.split() if s[0] == "a"][0]
LAST_ADDED = [int(s[1]) for s in SEQ.split() if s[0] == "a"][-1]
GP = 4
ZV = "".split()
ZF = "3".split()
AV = "".split()
WP = "0 1 2 3".split()
PS_KIND = dict(s.split(":") for s in "hvT:a e1:a g:a r:a zT:a selT:a cols:a out:a;a=8".split(";")[0].split())
PS_BUFS = dict((s.split("=")[0], int(s.split("=")[1])) for s in "hvT:a e1:a g:a r:a zT:a selT:a cols:a out:a;a=8".split(";")[1].split())


def tile_variableselectionnetwork_pb_kernel(
    tc, hv, x, sel_w, vW1, vb1, vW4, vb4, vW5, vb5, vlng, vlnb, out
):
    nc = tc.nc
    with ExitStack() as ctx:
        consts = ctx.enter_context(tc.tile_pool(name="consts", bufs=1))
        loads = ctx.enter_context(tc.tile_pool(name="loads", bufs=1))
        quantised = ctx.enter_context(tc.tile_pool(name="quantised", bufs=1))
        staging = ctx.enter_context(tc.tile_pool(name="staging", bufs=3))
        work = ctx.enter_context(tc.tile_pool(name="work", bufs=2))
        psum = ctx.enter_context(tc.psum_pool(name="psum", bufs=6))

        vector_rows = consts.tile([P, P], BF16)
        nc.vector.memset(vector_rows[:], 0.0)
        b1_cols = consts.tile([P, NV * PACK], BF16)
        b1_rows = consts.tile([P, D], BF16)
        nc.vector.memset(b1_rows[:], 0.0)

        def load_vectors():
            nc.sync.dma_start(out=b1_rows[0:NV, :], in_=vb1[:, :])
            for i, vec in enumerate((vb4, vb5, vlng, vlnb)):
                nc.sync.dma_start(
                    out=vector_rows[NV * CHUNKS * i : NV * CHUNKS * (i + 1), :],
                    in_=vec.rearrange("n (c p) -> (n c) p", p=P),
                )

        def load_rows(src, name):
            tiles = []
            for h in range(HALVES):
                t = loads.tile([P, NV * D], BF16, name="%s%d" % (name, h))
                nc.sync.dma_start(
                    out=t[:], in_=src[h * P : (h + 1) * P].rearrange("b n d -> b (n d)")
                )
                tiles.append(t)
            return tiles

        def load_weight(w, n, name):
            t = loads.tile([P, PACK, D], BF16, name="%s_raw%d" % (name, n))
            nc.sync.dma_start(out=t[:], in_=w[n].rearrange("(p t) c -> p t c", t=PACK))
            return t

        w1_raw, w4_raw, w5_raw = {}, {}, {}
        acts = {}
        for item in "w10 w40 w50 w11 vec hv w41 w51 w12 x w42 w52 w13 sel w43 w53".split():
            if item == "vec":
                load_vectors()
            elif item == "hv":
                acts["hv"] = load_rows(hv, "hv")
            elif item == "x":
                acts["x"] = load_rows(x, "x")
            elif item == "sel":
                acts["sel"] = load_rows(sel_w, "sel")
            else:
                n = int(item[2])
                {"w1": w1_raw, "w4": w4_raw, "w5": w5_raw}[item[:2]][n] = load_weight({"w1": vW1, "w4": vW4, "w5": vW5}[item[:2]], n, item[:2])
        hv_sb, x_sb, sel_sb = acts["hv"], acts["x"], acts["sel"]

        ident = consts.tile([P, P], F32)
        make_identity(nc, ident[:])
        ident_bf16 = consts.tile([P, P], BF16)
        make_identity(nc, ident_bf16[:])
        minus_half = consts.tile([P, HALVES], F32)
        nc.gpsimd.memset(minus_half[:], -0.5)

        table_warm = consts.tile([P, 1], F32)
        nc.scalar.activation(out=table_warm[:], in_=minus_half[:, 0:1], func=ACT.Sigmoid)

        vector_cols = consts.tile([P, COLUMN_VECTORS * NV * CHUNKS], F32)

        def column(i, n, c):
            j = NV * CHUNKS * i + CHUNKS * n + c
            return vector_cols[:, j : j + 1]

        mean_var = consts.tile([P, NV * HALVES, 2], F32)
        neg_mean = consts.tile([P, NV * HALVES], F32)
        var_eps = consts.tile([P, NV * HALVES], F32)
        rstd = consts.tile([P, NV * HALVES], F32)
        neg_mean_rstd = consts.tile([P, NV * HALVES], F32)
        rstd_late = consts.tile([P, NV * HALVES], F32)
        neg_mean_rstd_late = consts.tile([P, NV * HALVES], F32)
        table_warm_late = consts.tile([P, 1], F32)

        out_ps = []

        def quantise_weight(raw, name, n):
            grouped = staging.tile([P, D, PACK], BF16, tag="grouped", bufs=6, align_bytes=64)
            if name == "w1":
                dst = grouped[:].rearrange("p (u m) t -> p m t u", u=PACK)
                src = raw[:].rearrange("p t (m u) -> p m t u", u=PACK)
            else:
                dst = grouped[:].rearrange("p (c i) t -> p c t i", i=8)
                src = raw[:].rearrange("p t (c i) -> p c t i", i=8)
            if (name, n) in GPSIMD_REGROUPS:
                if name != "w1":
                    dst = grouped[:].rearrange("p (u m) t -> p u m t", u=GP)
                    src = raw[:].rearrange("p t (u m) -> p u m t", u=GP)
                for u in range(dst.shape[1]):
                    nc.gpsimd.tensor_scalar(
                        out=dst[:, u], in0=src[:, u], scalar1=1.0, scalar2=0.0, op0=ALU.mult, op1=ALU.add
                    )
            elif (name, n) in VECTOR_REGROUPS:
                nc.vector.tensor_copy(out=dst, in_=src)
            else:
                nc.scalar.copy(out=dst, in_=src)
            codes = quantised.tile([P, D], U32, name="%s_codes%d" % (name, n), align_bytes=64)
            scales = quantised.tile([P, D], U8, name="%s_scales%d" % (name, n), align_bytes=64)
            nc.vector.quantize_mx(
                out=codes[:].bitcast(FP8X4),
                scales=scales[:],
                in_=grouped[:].rearrange("p c t -> p (c t)"),
            )
            return codes, scales

        def quantise_hv(n):
            words_per_row = D // 2
            hvT_ps = psum.tile([P, 2, B], F32, name="hvT_ps", tag=PS_KIND["hvT"], bufs=PS_BUFS[PS_KIND["hvT"]])
            for u in range(2):
                for h in range(HALVES):
                    first = n * words_per_row
                    nc.tensor.transpose(
                        hvT_ps[:, u, h * P : (h + 1) * P],
                        hv_sb[h][:].bitcast(F32)[:, first + u : first + words_per_row : 2],
                        ident[:],
                    )
            grouped = staging.tile([P, B * PACK], BF16, tag="hv_grouped", align_bytes=64)
            nc.scalar.copy(
                out=grouped[:].bitcast(F32).rearrange("p (b u) -> p b u", u=2),
                in_=hvT_ps[:].rearrange("p u b -> p b u"),
            )
            codes = quantised.tile([P, B], U32, name="hv_codes%d" % n, align_bytes=64)
            scales = quantised.tile([P, B], U8, name="hv_scales%d" % n, align_bytes=64)
            nc.vector.quantize_mx(out=codes[:].bitcast(FP8X4), scales=scales[:], in_=grouped[:])
            return codes, scales

        def first_product(n, w1_q, hv_q):
            grouped = staging.tile([P, B, PACK], BF16, tag="e1_grouped", align_bytes=64)
            for h in range(HALVES):
                rows = slice(h * P, (h + 1) * P)
                e1_ps = psum.tile([P, PACK, P], F32, name="e1_ps", tag=PS_KIND["e1"], bufs=PS_BUFS[PS_KIND["e1"]])
                for t in range(PACK):
                    feats = slice(t * P, (t + 1) * P)
                    nc.tensor.matmul_mx(
                        out=e1_ps[:, t, :],
                        lhsT=w1_q[0][:, feats].bitcast(FP8X4),
                        lhsT_scale=w1_q[1][:, feats],
                        rhs=hv_q[0][:, rows].bitcast(FP8X4),
                        rhs_scale=hv_q[1][:, rows],
                        start=True,
                        stop=True,
                    )
                first = PACK * n
                nc.vector.tensor_tensor(
                    out=grouped[:, rows, :],
                    in0=e1_ps[:].rearrange("p t b -> p b t"),
                    in1=b1_cols[:, first : first + PACK].unsqueeze(1).to_broadcast([P, P, PACK]),
                    op=ALU.add,
                )
            codes = staging.tile([P, B], U32, tag="e1_codes", align_bytes=64)
            scales = staging.tile([P, B], U8, tag="e1_scales", align_bytes=64)
            nc.vector.quantize_mx(
                out=codes[:].bitcast(FP8X4),
                scales=scales[:],
                in_=grouped[:].rearrange("p b t -> p (b t)"),
            )
            return codes, scales

        def gate(n, e1_q, w4_q, w5_q):
            gvT = work.tile([P, CHUNKS, B], F32, tag="gvT", bufs=NV)
            for pair in range(CHUNKS // 2):
                banks = []
                for w_q in (w4_q, w5_q):
                    g_ps = psum.tile([P, 2, B], F32, name="g_ps", tag=PS_KIND["g"], bufs=PS_BUFS[PS_KIND["g"]])
                    for i in range(2):
                        c = 2 * pair + i
                        feats = slice(c * P, (c + 1) * P)
                        nc.tensor.matmul_mx(
                            out=g_ps[:, i, :],
                            lhsT=w_q[0][:, feats].bitcast(FP8X4),
                            lhsT_scale=w_q[1][:, feats],
                            rhs=e1_q[0][:].bitcast(FP8X4),
                            rhs_scale=e1_q[1][:],
                            start=True,
                            stop=True,
                        )
                    banks.append(g_ps)
                sig = work.tile([P, 2, B], F32, tag="sig", bufs=4)
                for i in range(2):
                    c = 2 * pair + i
                    nc.scalar.activation(
                        out=sig[:, i, :], in_=banks[0][:, i, :], func=ACT.Sigmoid, bias=column(0, n, c)
                    )
                    nc.vector.scalar_tensor_tensor(
                        out=gvT[:, c, :],
                        in0=banks[1][:, i, :],
                        scalar=column(1, n, c),
                        in1=sig[:, i, :],
                        op0=ALU.add,
                        op1=ALU.mult,
                    )
            if n == NV - 1:
                nc.scalar.activation(out=table_warm_late[:], in_=sig[:, 1, 0:1], func=ACT.Abs_reciprocal_sqrt)
            return gvT

        def standardise(n, gvT):
            feats = slice(n * D, (n + 1) * D)
            cols = slice(n * HALVES, (n + 1) * HALVES)
            r_ps = []
            for h in range(HALVES):
                r_h = psum.tile([P, D], F32, name="r_ps", tag=PS_KIND["r"], bufs=PS_BUFS[PS_KIND["r"]])
                nc.tensor.matmul(
                    out=r_h[:], lhsT=ident_bf16[:], rhs=x_sb[h][:, feats], start=True, stop=False
                )
                for c in range(CHUNKS):
                    nc.tensor.matmul(
                        out=r_h[:, c * P : (c + 1) * P],
                        lhsT=gvT[:, c, h * P : (h + 1) * P],
                        rhs=ident[:],
                        is_transpose=True,
                        start=False,
                        stop=(c == CHUNKS - 1),
                    )
                r_ps.append(r_h)
                stats = work.tile([P, STATS], F32, tag="stats", bufs=4)
                nc.vector.bn_stats(out=stats[:], in_=r_h[:])
                nc.vector.bn_aggr(out=mean_var[:, n * HALVES + h, :], in_=stats[:])
            nc.vector.tensor_scalar(
                out=var_eps[:, cols], in0=mean_var[:, cols, 1],
                scalar1=1.0, scalar2=EPS, op0=ALU.mult, op1=ALU.add,
            )
            if str(n) not in ZF:
                nc.vector.tensor_scalar(
                    out=neg_mean[:, cols], in0=mean_var[:, cols, 0],
                    scalar1=-1.0, scalar2=0.0, op0=ALU.mult, op1=ALU.add,
                )
            if n >= NV - 2:
                nc.scalar.activation(out=rstd_late[:, cols], in_=var_eps[:, cols], func=ACT.Abs_reciprocal_sqrt)
            else:
                nc.gpsimd.tensor_tensor(
                    out=rstd[:, cols], in0=var_eps[:, cols], in1=minus_half[:], op=ALU.pow
                )
            if str(n) not in ZF:
                if n >= NV - 2:
                    for h in range(HALVES):
                        j = n * HALVES + h
                        nc.scalar.activation(
                            out=neg_mean_rstd_late[:, j : j + 1], in_=neg_mean[:, j : j + 1], func=ACT.Identity,
                            scale=rstd_late[:, j : j + 1],
                        )
                else:
                    nc.gpsimd.tensor_tensor(
                        out=neg_mean_rstd[:, cols], in0=neg_mean[:, cols], in1=rstd[:, cols], op=ALU.mult
                    )
            rstd_n = rstd_late if n >= NV - 2 else rstd
            nms_n = neg_mean_rstd_late if n >= NV - 2 else neg_mean_rstd
            z = []
            for h in range(HALVES):
                j = n * HALVES + h
                z_h = work.tile([P, D], F32, tag="z", bufs=NV * HALVES)
                if str(n) in ZF or (str(n) in ZV and h == 1):
                    nc.vector.tensor_scalar(
                        out=z_h[:], in0=r_ps[h][:], scalar1=mean_var[:, j, 0:1], scalar2=rstd_n[:, j : j + 1],
                        op0=ALU.subtract, op1=ALU.mult,
                    )
                else:
                    nc.scalar.activation(
                        out=z_h[:], in_=r_ps[h][:], func=ACT.Identity,
                        scale=rstd_n[:, j : j + 1], bias=nms_n[:, j : j + 1],
                    )
                z.append(z_h)
            return z

        def weigh(n, z):
            selT_ps = psum.tile([P, CHUNKS, B], BF16, name="selT_ps", tag=PS_KIND["selT"], bufs=PS_BUFS[PS_KIND["selT"]])
            for c in range(CHUNKS):
                for h in range(HALVES):
                    first = n * D + c * P
                    nc.tensor.transpose(
                        selT_ps[:, c, h * P : (h + 1) * P], sel_sb[h][:, first : first + P], ident_bf16[:]
                    )
            yT = work.tile([P, CHUNKS, B], F32, tag="yT", bufs=2)
            for pair in range(CHUNKS // 2):
                zT_ps = psum.tile([P, 2, B], F32, name="zT_ps", tag=PS_KIND["zT"], bufs=PS_BUFS[PS_KIND["zT"]])
                for i in range(2):
                    c = 2 * pair + i
                    for h in range(HALVES):
                        nc.tensor.transpose(
                            zT_ps[:, i, h * P : (h + 1) * P], z[h][:, c * P : (c + 1) * P], ident[:]
                        )
                for i in range(2):
                    c = 2 * pair + i
                    if str(n) in AV and pair == 0:
                        nc.vector.tensor_scalar(
                            out=yT[:, c, :], in0=zT_ps[:, i, :], scalar1=column(2, n, c), scalar2=column(3, n, c),
                            op0=ALU.mult, op1=ALU.add,
                        )
                    else:
                        nc.scalar.activation(
                            out=yT[:, c, :], in_=zT_ps[:, i, :], func=ACT.Identity,
                            scale=column(2, n, c), bias=column(3, n, c),
                        )
            wT = work.tile([P, CHUNKS, B], F32, tag="wT", bufs=NV)
            if str(n) in WP:
                for pair in range(CHUNKS // 2):
                    cs = slice(2 * pair, 2 * pair + 2)
                    nc.vector.tensor_tensor(out=wT[:, cs, :], in0=yT[:, cs, :], in1=selT_ps[:, cs, :], op=ALU.mult)
            else:
                nc.vector.tensor_tensor(out=wT[:], in0=yT[:], in1=selT_ps[:], op=ALU.mult)
            return wT

        def add_up(n, wT):
            if not out_ps:
                for h in range(HALVES):
                    out_ps.append(psum.tile([P, D], F32, name="out_ps%d" % h, tag=PS_KIND["out"], bufs=PS_BUFS[PS_KIND["out"]]))
            for h in range(HALVES):
                for c in range(CHUNKS):
                    nc.tensor.matmul(
                        out=out_ps[h][:, c * P : (c + 1) * P],
                        lhsT=wT[:, c, h * P : (h + 1) * P],
                        rhs=ident[:],
                        is_transpose=True,
                        start=(n == FIRST_ADDED and c == 0),
                        stop=(n == LAST_ADDED and c == CHUNKS - 1),
                    )

        ctx.enter_context(tc.manual_schedule(engines={mybir.EngineType.PE}))
        cols_ps = psum.tile([P, P], BF16, name="cols_ps", tag=PS_KIND["cols"], bufs=PS_BUFS[PS_KIND["cols"]])
        nc.tensor.transpose(cols_ps[:], vector_rows[:], ident_bf16[:])
        nc.vector.tensor_copy(out=vector_cols[:], in_=cols_ps[:, 0 : COLUMN_VECTORS * NV * CHUNKS])
        b1_ps = psum.tile([P, PACK, P], BF16, name="b1_ps", tag=PS_KIND["cols"], bufs=PS_BUFS[PS_KIND["cols"]])
        for t in range(PACK):
            nc.tensor.transpose(b1_ps[:, t, :], b1_rows[:, t:D:PACK], ident_bf16[:])
        nc.vector.tensor_copy(
            out=b1_cols[:].rearrange("p (n t) -> p n t", t=PACK),
            in_=b1_ps[:, :, 0:NV].rearrange("p t n -> p n t"),
        )
        w_q, e1_q, gvT, z, wT = {}, {}, {}, {}, {}

        hv_q = {}
        raws = {"w1": w1_raw, "w4": w4_raw, "w5": w5_raw}
        def do_step(op, n):
            if op in raws:
                w_q[op, n] = quantise_weight(raws[op][n], op, n)
            elif op == "hv":
                hv_q[n] = quantise_hv(n)
            elif op == "s":
                e1_q[n] = first_product(n, w_q["w1", n], hv_q[n])
            elif op == "g":
                gvT[n] = gate(n, e1_q[n], w_q["w4", n], w_q["w5", n])
            elif op == "r":
                z[n] = standardise(n, gvT[n])
            elif op == "b":
                wT[n] = weigh(n, z[n])
            elif op == "a":
                add_up(n, wT[n])

        for step in SEQ.split():
            op, n = step[:-1], int(step[-1])
            if op in HP:
                with tc.high_priority():
                    do_step(op, n)
            else:
                do_step(op, n)

        for h in range(HALVES):
            result = work.tile([P, D], F32, tag="result")
            if h == 0:
                nc.scalar.copy(out=result[:], in_=out_ps[h][:])
            else:
                nc.vector.tensor_copy(out=result[:], in_=out_ps[h][:])
            nc.sync.dma_start(out=out[h * P : (h + 1) * P, :], in_=result[:])
